import numpy as np
import ml_dtypes


def mxq(x, axis, fmt="e4m3"):
    dtype, down = {"e4m3": (ml_dtypes.float8_e4m3fn, 7), "e5m2": (ml_dtypes.float8_e5m2, 14)}[fmt]
    v = np.moveaxis(np.asarray(x, np.float32).astype(ml_dtypes.bfloat16).astype(np.float64), axis, -1)
    blocks = v.reshape(v.shape[:-1] + (-1, 32))
    amax = np.abs(blocks).max(-1, keepdims=True)
    byte = np.maximum(np.where(amax > 0, np.frexp(amax)[1] - 1 + 127, 0) - down, 1)
    scale = np.exp2(byte - 127.0)
    codes = (blocks / scale).astype(np.float32).astype(dtype).astype(np.float64)
    return np.moveaxis((codes * scale).reshape(v.shape), -1, axis)


WIDE = False


def mx_kscale(k):
    if not WIDE:
        return np.ones(k)
    levels = np.array([10, -10, 5, -5, 0])
    a = np.random.permutation(np.resize(levels, k // 512 * 4)).reshape(k // 512, 4)
    idx = np.arange(k)
    return np.exp2(a[idx // 512, idx % 128 // 32])


BF16 = ml_dtypes.bfloat16


def bf(x):
    return np.asarray(x, np.float32).astype(BF16)


def f64(x):
    return np.asarray(x).astype(np.float64)


B, D_IN, D_H, W_RANK, U_RANK = 1024, 1024, 2048, 512, 512


def sigmoid(v):
    return 1.0 / (1.0 + np.exp(-v))


def setup_inputs():
    s, t = mx_kscale(W_RANK), mx_kscale(U_RANK)
    return {
        "wx_r": bf(np.random.standard_normal((B, W_RANK)) * s),
        "uh_r": bf(np.random.standard_normal((B, U_RANK)) * t),
        "state": bf(np.random.standard_normal((B, D_H))),
        "W2": bf(np.random.standard_normal((D_H, W_RANK)) * 0.7 / np.sqrt(W_RANK) / s),
        "U2": bf(np.random.standard_normal((D_H, U_RANK)) * 0.7 / np.sqrt(U_RANK) / t),
        "bias_gate": bf(1.0 + 0.5 * np.random.standard_normal((1, D_H))),
        "bias_update": bf(1.0 + 0.5 * np.random.standard_normal((1, D_H))),
        "zeta": bf(1.0 + 0.1 * np.random.standard_normal((1, 1))),
        "nu": bf(-1.5 + 0.1 * np.random.standard_normal((1, 1))),
    }


def reference(wx_r, uh_r, state, W2, U2, bias_gate, bias_update, zeta, nu):
    wx = mxq(f64(wx_r), 1, "e4m3") @ mxq(f64(W2), 1, "e4m3").T
    uh = mxq(f64(uh_r), 1, "e4m3") @ mxq(f64(U2), 1, "e4m3").T
    pre = wx + uh
    z = sigmoid(pre + f64(bias_gate))
    h_cand = np.tanh(pre + f64(bias_update))
    return z * f64(state) + (sigmoid(f64(zeta)) * (1.0 - z) + sigmoid(f64(nu))) * h_cand

@@ -1,0 +1,252 @@
+from contextlib import ExitStack
+
+import concourse.mybir as mybir
+from concourse.masks import make_identity
+
+F32 = mybir.dt.float32
+BF16 = mybir.dt.bfloat16
+U32 = mybir.dt.uint32
+U8 = mybir.dt.uint8
+FP8X4 = mybir.dt.float8_e4m3fn_x4
+ACT = mybir.ActivationFunctionType
+ALU = mybir.AluOpType
+
+P = 128
+PACK = 4
+BATCH, HIDDEN, RANK = 1024, 2048, 512
+WORD_HALVES = 2
+STREAMS = 2
+ROWS_PER_PARTITION = BATCH // P
+HALF_CHUNKS = 4
+HALVES = ROWS_PER_PARTITION // HALF_CHUNKS
+HIDDEN_TILES = HIDDEN // P
+GROUP_TILES = 4
+GROUPS = HIDDEN_TILES // GROUP_TILES
+STORE_TILES = 2
+UNITS = HIDDEN_TILES * HALVES
+TILES_AHEAD = 2
+
+FLOPS = 2 * BATCH * HIDDEN * RANK * STREAMS
+
+
+def tile_fastgrnncudacell_pa_kernel(
+    tc, wx_r, uh_r, state, W2, U2, bias_gate, bias_update, zeta, nu, out
+):
+    nc = tc.nc
+    assert tuple(wx_r.shape) == (BATCH, RANK) and tuple(W2.shape) == (HIDDEN, RANK)
+
+    act_views = [x.rearrange("(r i) k -> r i k", i=ROWS_PER_PARTITION) for x in (wx_r, uh_r)]
+    state_view = state.rearrange("(r i) d -> r i d", i=ROWS_PER_PARTITION)
+    out_view = out.rearrange("(r i) d -> r i d", i=ROWS_PER_PARTITION)
+    weight_views = [w.rearrange("(t m) k -> m t k", m=P) for w in (W2, U2)]
+
+    with ExitStack() as ctx:
+        ctx.enter_context(tc.manual_schedule())
+        keep = ctx.enter_context(tc.tile_pool(name="keep", bufs=1))
+        stage = ctx.enter_context(tc.tile_pool(name="stage", bufs=6))
+        gates_pool = ctx.enter_context(tc.tile_pool(name="gates", bufs=3))
+        mix_pool = ctx.enter_context(tc.tile_pool(name="mix", bufs=2))
+        out_pool = ctx.enter_context(tc.tile_pool(name="outs", bufs=3))
+        banks = ctx.enter_context(tc.psum_pool(name="banks", bufs=8))
+
+        identity = keep.tile([P, P], F32, name="identity")
+        make_identity(nc, identity[:])
+
+        bias_rows = keep.tile([P, P], BF16, name="bias_rows")
+        nc.vector.memset(bias_rows[:], 0.0)
+        for n, bias in enumerate((bias_gate, bias_update)):
+            nc.scalar.dma_start(
+                out=bias_rows[n * HIDDEN_TILES : (n + 1) * HIDDEN_TILES, :],
+                in_=bias.rearrange("o (t m) -> (o t) m", m=P),
+            )
+        zeta_col = keep.tile([P, 1], BF16, name="zeta_col")
+        nu_col = keep.tile([P, 1], BF16, name="nu_col")
+        nc.scalar.dma_start(out=zeta_col[:], in_=zeta.to_broadcast([P, 1]))
+        nc.scalar.dma_start(out=nu_col[:], in_=nu.to_broadcast([P, 1]))
+
+        act_raw = {}
+        weight_raw = {}
+        state_sb = {}
+
+        def load_acts(half):
+            for s in range(STREAMS):
+                raw = keep.tile([P, HALF_CHUNKS, RANK], BF16, name="act_raw_%d_%d" % (s, half))
+                chunks = slice(half * HALF_CHUNKS, (half + 1) * HALF_CHUNKS)
+                nc.sync.dma_start(out=raw[:], in_=act_views[s][:, chunks, :])
+                act_raw[(s, half)] = raw
+
+        def load_weights(group):
+            for s in range(STREAMS):
+                raw = keep.tile([P, GROUP_TILES, RANK], BF16, name="weight_raw_%d_%d" % (s, group))
+                tiles = slice(group * GROUP_TILES, (group + 1) * GROUP_TILES)
+                nc.sync.dma_start(out=raw[:], in_=weight_views[s][:, tiles, :])
+                weight_raw[(s, group)] = raw
+
+        def load_state(group):
+            part = keep.tile([P, ROWS_PER_PARTITION, GROUP_TILES * P], BF16, name="state_%d" % group)
+            cols = slice(group * GROUP_TILES * P, (group + 1) * GROUP_TILES * P)
+            nc.sync.dma_start(out=part[:], in_=state_view[:, :, cols])
+            state_sb[group] = part
+
+        load_acts(0)
+        load_weights(0)
+        load_acts(1)
+        load_state(0)
+        for group in range(1, GROUPS):
+            load_weights(group)
+            load_state(group)
+
+        sig_zeta = keep.tile([P, 1], F32, name="sig_zeta")
+        sig_nu = keep.tile([P, 1], F32, name="sig_nu")
+        nc.scalar.activation(out=sig_zeta[:], in_=zeta_col[:], func=ACT.Sigmoid)
+        nc.scalar.activation(out=sig_nu[:], in_=nu_col[:], func=ACT.Sigmoid)
+
+        act_codes = [keep.tile([P, BATCH], U32, name="act_codes_%d" % s, align_bytes=64) for s in range(STREAMS)]
+        act_scales = [keep.tile([P, BATCH], U8, name="act_scales_%d" % s, align_bytes=64) for s in range(STREAMS)]
+        weight_codes = keep.tile([P, STREAMS * HIDDEN], U32, name="weight_codes", align_bytes=64)
+        weight_scales = keep.tile([P, STREAMS * HIDDEN], U8, name="weight_scales", align_bytes=64)
+
+        def turn_rows(row_tiles, copy):
+            turned = banks.tile([P, WORD_HALVES, 2 * P], F32, tag="bank")
+            for n, rows in enumerate(row_tiles):
+                words = rows.bitcast(F32)
+                for h in range(WORD_HALVES):
+                    nc.tensor.transpose(
+                        turned[:, h, n * P : (n + 1) * P], words[:, h * P : (h + 1) * P], identity[:]
+                    )
+            grouped = stage.tile([P, 2 * P, PACK], BF16, align_bytes=64)
+            copy(out=grouped[:].bitcast(F32), in_=turned[:].rearrange("p h r -> p r h"))
+            return grouped
+
+        def quantise(grouped, codes, scales):
+            nc.vector.quantize_mx(
+                out=codes.bitcast(FP8X4), scales=scales, in_=grouped[:].rearrange("p r t -> p (r t)")
+            )
+
+        def quantise_acts(half):
+            grouped = {}
+            for s, copy in enumerate((nc.vector.tensor_copy, nc.scalar.copy)):
+                for pair in range(HALF_CHUNKS // 2):
+                    raw = act_raw[(s, half)]
+                    grouped[(s, pair)] = turn_rows([raw[:, 2 * pair, :], raw[:, 2 * pair + 1, :]], copy)
+            for s in range(STREAMS):
+                for pair in range(HALF_CHUNKS // 2):
+                    first = (half * HALF_CHUNKS + 2 * pair) * P
+                    cols = slice(first, first + 2 * P)
+                    quantise(grouped[(s, pair)], act_codes[s][:, cols], act_scales[s][:, cols])
+
+        def turn_weights(t):
+            group, member = divmod(t, GROUP_TILES)
+            return turn_rows([weight_raw[(s, group)][:, member, :] for s in range(STREAMS)], nc.scalar.copy)
+
+        def quantise_weights(t, grouped):
+            cols = slice(t * STREAMS * P, (t + 1) * STREAMS * P)
+            quantise(grouped, weight_codes[:, cols], weight_scales[:, cols])
+
+        pre = {}
+        cand = {}
+        gate = {}
+        cand_rows = {}
+        gate_rows = {}
+        drop = {}
+        gated = {}
+        out_tiles = {}
+
+        def products(u):
+            t, half = divmod(u, HALVES)
+            pre[u] = banks.tile([P, HALF_CHUNKS * P], F32, name="pre", tag="bank")
+            b_cols = slice(half * HALF_CHUNKS * P, (half + 1) * HALF_CHUNKS * P)
+            for s in range(STREAMS):
+                w_cols = slice((t * STREAMS + s) * P, (t * STREAMS + s + 1) * P)
+                nc.tensor.matmul_mx(
+                    out=pre[u][:],
+                    lhsT=weight_codes[:, w_cols].bitcast(FP8X4),
+                    lhsT_scale=weight_scales[:, w_cols],
+                    rhs=act_codes[s][:, b_cols].bitcast(FP8X4),
+                    rhs_scale=act_scales[s][:, b_cols],
+                    start=(s == 0),
+                    stop=(s == STREAMS - 1),
+                )
+
+        def gates(u):
+            t = u // HALVES
+            cand[u] = gates_pool.tile([P, HALF_CHUNKS * P], F32, name="cand")
+            gate[u] = gates_pool.tile([P, HALF_CHUNKS * P], F32, name="gate")
+            nc.scalar.activation(
+                out=cand[u][:], in_=pre[u][:], func=ACT.Tanh,
+                bias=bias_cols[:, HIDDEN_TILES + t : HIDDEN_TILES + t + 1], scale=1.0,
+            )
+            nc.scalar.activation(
+                out=gate[u][:], in_=pre[u][:], func=ACT.Sigmoid, bias=bias_cols[:, t : t + 1], scale=1.0
+            )
+
+        def turn_back(u):
+            cand_rows[u] = banks.tile([P, HALF_CHUNKS, P], F32, name="cand_rows", tag="bank")
+            gate_rows[u] = banks.tile([P, HALF_CHUNKS, P], F32, name="gate_rows", tag="bank")
+            for turned, source in ((cand_rows[u], cand[u]), (gate_rows[u], gate[u])):
+                for i in range(HALF_CHUNKS):
+                    nc.tensor.transpose(turned[:, i, :], source[:, i * P : (i + 1) * P], identity[:])
+
+        def mix_drop(u):
+            t, half = divmod(u, HALVES)
+            group, member = divmod(t, GROUP_TILES)
+            chunks = slice(half * HALF_CHUNKS, (half + 1) * HALF_CHUNKS)
+            drop[u] = mix_pool.tile([P, HALF_CHUNKS, P], F32, name="drop")
+            nc.vector.scalar_tensor_tensor(
+                out=drop[u][:], in0=cand_rows[u][:], scalar=sig_zeta[:, 0:1],
+                in1=state_sb[group][:, chunks, member * P : (member + 1) * P],
+                op0=ALU.mult, op1=ALU.subtract,
+            )
+
+        def mix_gate(u):
+            gated[u] = mix_pool.tile([P, HALF_CHUNKS, P], F32, name="gated")
+            nc.vector.tensor_tensor(out=gated[u][:], in0=gate_rows[u][:], in1=drop[u][:], op=ALU.mult)
+
+        def mix_out(u):
+            t, half = divmod(u, HALVES)
+            store, member = divmod(t, STORE_TILES)
+            chunks = slice(half * HALF_CHUNKS, (half + 1) * HALF_CHUNKS)
+            if member == 0 and half == 0:
+                out_tiles[store] = out_pool.tile([P, ROWS_PER_PARTITION, STORE_TILES * P], F32, name="out_tile")
+            nc.vector.scalar_tensor_tensor(
+                out=out_tiles[store][:, chunks, member * P : (member + 1) * P],
+                in0=cand_rows[u][:], scalar=sig_sum[:, 0:1], in1=gated[u][:],
+                op0=ALU.mult, op1=ALU.subtract,
+            )
+            if member == STORE_TILES - 1:
+                cols = slice(store * STORE_TILES * P, (store + 1) * STORE_TILES * P)
+                nc.sync.dma_start(out=out_view[:, chunks, cols], in_=out_tiles[store][:, chunks, :])
+
+        quantise_acts(0)
+
+        bias_rows_f32 = keep.tile([P, P], F32, name="bias_rows_f32")
+        nc.vector.tensor_copy(out=bias_rows_f32[:], in_=bias_rows[:])
+        bias_turned = banks.tile([P, P], F32, tag="bank")
+        nc.tensor.transpose(bias_turned[:], bias_rows_f32[:], identity[:])
+        bias_cols = keep.tile([P, 2 * HIDDEN_TILES], F32, name="bias_cols")
+        nc.vector.tensor_copy(out=bias_cols[:], in_=bias_turned[:, 0 : 2 * HIDDEN_TILES])
+        sig_sum = keep.tile([P, 1], F32, name="sig_sum")
+        nc.vector.tensor_add(out=sig_sum[:], in0=sig_zeta[:], in1=sig_nu[:])
+
+        quantise_weights(0, turn_weights(0))
+        products(0)
+        gates(0)
+        quantise_acts(1)
+        quantise_weights(1, turn_weights(1))
+
+        grouped_ahead = {}
+        for u in range(UNITS):
+            t_ahead = u // HALVES + TILES_AHEAD
+            if u + 1 < UNITS:
+                products(u + 1)
+                gates(u + 1)
+            turn_back(u)
+            if u % HALVES == 0 and t_ahead < HIDDEN_TILES:
+                grouped_ahead[t_ahead] = turn_weights(t_ahead)
+            mix_drop(u)
+            if u > 0:
+                mix_out(u - 1)
+            mix_gate(u)
+            if u % HALVES == 1 and t_ahead < HIDDEN_TILES:
+                quantise_weights(t_ahead, grouped_ahead[t_ahead])
+        mix_out(UNITS - 1)

@@ -41,7 +41,6 @@ def tile_fastgrnncudacell_pa_kernel(
     weight_views = [w.rearrange("(t m) k -> m t k", m=P) for w in (W2, U2)]
 
     with ExitStack() as ctx:
-        ctx.enter_context(tc.manual_schedule())
         keep = ctx.enter_context(tc.tile_pool(name="keep", bufs=1))
         stage = ctx.enter_context(tc.tile_pool(name="stage", bufs=6))
         gates_pool = ctx.enter_context(tc.tile_pool(name="gates", bufs=3))

@@ -20,11 +20,11 @@ ROWS_PER_PARTITION = BATCH // P
 HALF_CHUNKS = 4
 HALVES = ROWS_PER_PARTITION // HALF_CHUNKS
 HIDDEN_TILES = HIDDEN // P
-GROUP_TILES = 4
-GROUPS = HIDDEN_TILES // GROUP_TILES
-STORE_TILES = 2
+WEIGHT_LOAD_TILES = 2
+STATE_LOAD_TILES = 4
 UNITS = HIDDEN_TILES * HALVES
 TILES_AHEAD = 2
+OUT_LAG = 2
 
 FLOPS = 2 * BATCH * HIDDEN * RANK * STREAMS
 
@@ -41,11 +41,12 @@ def tile_fastgrnncudacell_pa_kernel(
     weight_views = [w.rearrange("(t m) k -> m t k", m=P) for w in (W2, U2)]
 
     with ExitStack() as ctx:
+        ctx.enter_context(tc.manual_schedule())
         keep = ctx.enter_context(tc.tile_pool(name="keep", bufs=1))
         stage = ctx.enter_context(tc.tile_pool(name="stage", bufs=6))
         gates_pool = ctx.enter_context(tc.tile_pool(name="gates", bufs=3))
-        mix_pool = ctx.enter_context(tc.tile_pool(name="mix", bufs=2))
-        out_pool = ctx.enter_context(tc.tile_pool(name="outs", bufs=3))
+        mix_pool = ctx.enter_context(tc.tile_pool(name="mix", bufs=4))
+        out_pool = ctx.enter_context(tc.tile_pool(name="outs", bufs=6))
         banks = ctx.enter_context(tc.psum_pool(name="banks", bufs=8))
 
         identity = keep.tile([P, P], F32, name="identity")
@@ -74,26 +75,28 @@ def tile_fastgrnncudacell_pa_kernel(
                 nc.sync.dma_start(out=raw[:], in_=act_views[s][:, chunks, :])
                 act_raw[(s, half)] = raw
 
-        def load_weights(group):
+        def load_weights(n):
             for s in range(STREAMS):
-                raw = keep.tile([P, GROUP_TILES, RANK], BF16, name="weight_raw_%d_%d" % (s, group))
-                tiles = slice(group * GROUP_TILES, (group + 1) * GROUP_TILES)
+                raw = keep.tile([P, WEIGHT_LOAD_TILES, RANK], BF16, name="weight_raw_%d_%d" % (s, n))
+                tiles = slice(n * WEIGHT_LOAD_TILES, (n + 1) * WEIGHT_LOAD_TILES)
                 nc.sync.dma_start(out=raw[:], in_=weight_views[s][:, tiles, :])
-                weight_raw[(s, group)] = raw
+                weight_raw[(s, n)] = raw
 
-        def load_state(group):
-            part = keep.tile([P, ROWS_PER_PARTITION, GROUP_TILES * P], BF16, name="state_%d" % group)
-            cols = slice(group * GROUP_TILES * P, (group + 1) * GROUP_TILES * P)
+        def load_state(n):
+            part = keep.tile([P, ROWS_PER_PARTITION, STATE_LOAD_TILES * P], BF16, name="state_%d" % n)
+            cols = slice(n * STATE_LOAD_TILES * P, (n + 1) * STATE_LOAD_TILES * P)
             nc.sync.dma_start(out=part[:], in_=state_view[:, :, cols])
-            state_sb[group] = part
+            state_sb[n] = part
 
         load_acts(0)
         load_weights(0)
         load_acts(1)
         load_state(0)
-        for group in range(1, GROUPS):
-            load_weights(group)
-            load_state(group)
+        load_weights(1)
+        for n in range(1, HIDDEN_TILES // STATE_LOAD_TILES):
+            load_weights(2 * n)
+            load_weights(2 * n + 1)
+            load_state(n)
 
         sig_zeta = keep.tile([P, 1], F32, name="sig_zeta")
         sig_nu = keep.tile([P, 1], F32, name="sig_nu")
@@ -135,8 +138,8 @@ def tile_fastgrnncudacell_pa_kernel(
                     quantise(grouped[(s, pair)], act_codes[s][:, cols], act_scales[s][:, cols])
 
         def turn_weights(t):
-            group, member = divmod(t, GROUP_TILES)
-            return turn_rows([weight_raw[(s, group)][:, member, :] for s in range(STREAMS)], nc.scalar.copy)
+            n, member = divmod(t, WEIGHT_LOAD_TILES)
+            return turn_rows([weight_raw[(s, n)][:, member, :] for s in range(STREAMS)], nc.scalar.copy)
 
         def quantise_weights(t, grouped):
             cols = slice(t * STREAMS * P, (t + 1) * STREAMS * P)
@@ -149,7 +152,6 @@ def tile_fastgrnncudacell_pa_kernel(
         gate_rows = {}
         drop = {}
         gated = {}
-        out_tiles = {}
 
         def products(u):
             t, half = divmod(u, HALVES)
@@ -188,35 +190,36 @@ def tile_fastgrnncudacell_pa_kernel(
 
         def mix_drop(u):
             t, half = divmod(u, HALVES)
-            group, member = divmod(t, GROUP_TILES)
+            n, member = divmod(t, STATE_LOAD_TILES)
             chunks = slice(half * HALF_CHUNKS, (half + 1) * HALF_CHUNKS)
             drop[u] = mix_pool.tile([P, HALF_CHUNKS, P], F32, name="drop")
             nc.vector.scalar_tensor_tensor(
                 out=drop[u][:], in0=cand_rows[u][:], scalar=sig_zeta[:, 0:1],
-                in1=state_sb[group][:, chunks, member * P : (member + 1) * P],
+                in1=state_sb[n][:, chunks, member * P : (member + 1) * P],
                 op0=ALU.mult, op1=ALU.subtract,
             )
 
         def mix_gate(u):
             gated[u] = mix_pool.tile([P, HALF_CHUNKS, P], F32, name="gated")
-            nc.vector.tensor_tensor(out=gated[u][:], in0=gate_rows[u][:], in1=drop[u][:], op=ALU.mult)
+            if u % HALVES == 0:
+                nc.vector.tensor_tensor(out=gated[u][:], in0=gate_rows[u][:], in1=drop[u][:], op=ALU.mult)
+            else:
+                z_rows = mix_pool.tile([P, HALF_CHUNKS, P], F32, name="z_rows")
+                nc.scalar.copy(out=z_rows[:], in_=gate_rows[u][:])
+                nc.gpsimd.tensor_tensor(out=gated[u][:], in0=z_rows[:], in1=drop[u][:], op=ALU.mult)
 
         def mix_out(u):
             t, half = divmod(u, HALVES)
-            store, member = divmod(t, STORE_TILES)
             chunks = slice(half * HALF_CHUNKS, (half + 1) * HALF_CHUNKS)
-            if member == 0 and half == 0:
-                out_tiles[store] = out_pool.tile([P, ROWS_PER_PARTITION, STORE_TILES * P], F32, name="out_tile")
+            out_tile = out_pool.tile([P, HALF_CHUNKS, P], F32, name="out_tile")
             nc.vector.scalar_tensor_tensor(
-                out=out_tiles[store][:, chunks, member * P : (member + 1) * P],
-                in0=cand_rows[u][:], scalar=sig_sum[:, 0:1], in1=gated[u][:],
+                out=out_tile[:], in0=cand_rows[u][:], scalar=sig_sum[:, 0:1], in1=gated[u][:],
                 op0=ALU.mult, op1=ALU.subtract,
             )
-            if member == STORE_TILES - 1:
-                cols = slice(store * STORE_TILES * P, (store + 1) * STORE_TILES * P)
-                nc.sync.dma_start(out=out_view[:, chunks, cols], in_=out_tiles[store][:, chunks, :])
+            nc.sync.dma_start(out=out_view[:, chunks, t * P : (t + 1) * P], in_=out_tile[:])
 
         quantise_acts(0)
+        quantise_weights(0, turn_weights(0))
 
         bias_rows_f32 = keep.tile([P, P], F32, name="bias_rows_f32")
         nc.vector.tensor_copy(out=bias_rows_f32[:], in_=bias_rows[:])
@@ -227,25 +230,25 @@ def tile_fastgrnncudacell_pa_kernel(
         sig_sum = keep.tile([P, 1], F32, name="sig_sum")
         nc.vector.tensor_add(out=sig_sum[:], in0=sig_zeta[:], in1=sig_nu[:])
 
-        quantise_weights(0, turn_weights(0))
         products(0)
         gates(0)
         quantise_acts(1)
         quantise_weights(1, turn_weights(1))
 
         grouped_ahead = {}
-        for u in range(UNITS):
+        for u in range(UNITS + OUT_LAG):
             t_ahead = u // HALVES + TILES_AHEAD
             if u + 1 < UNITS:
                 products(u + 1)
                 gates(u + 1)
-            turn_back(u)
-            if u % HALVES == 0 and t_ahead < HIDDEN_TILES:
-                grouped_ahead[t_ahead] = turn_weights(t_ahead)
-            mix_drop(u)
-            if u > 0:
-                mix_out(u - 1)
-            mix_gate(u)
-            if u % HALVES == 1 and t_ahead < HIDDEN_TILES:
-                quantise_weights(t_ahead, grouped_ahead[t_ahead])
-        mix_out(UNITS - 1)
+            if u < UNITS:
+                turn_back(u)
+                if u % HALVES == 0 and t_ahead < HIDDEN_TILES:
+                    grouped_ahead[t_ahead] = turn_weights(t_ahead)
+                mix_drop(u)
+            if u >= OUT_LAG:
+                mix_out(u - OUT_LAG)
+            if u < UNITS:
+                mix_gate(u)
+                if u % HALVES == 1 and t_ahead < HIDDEN_TILES:
+                    quantise_weights(t_ahead, grouped_ahead[t_ahead])

@@ -201,12 +201,7 @@ def tile_fastgrnncudacell_pa_kernel(
 
         def mix_gate(u):
             gated[u] = mix_pool.tile([P, HALF_CHUNKS, P], F32, name="gated")
-            if u % HALVES == 0:
-                nc.vector.tensor_tensor(out=gated[u][:], in0=gate_rows[u][:], in1=drop[u][:], op=ALU.mult)
-            else:
-                z_rows = mix_pool.tile([P, HALF_CHUNKS, P], F32, name="z_rows")
-                nc.scalar.copy(out=z_rows[:], in_=gate_rows[u][:])
-                nc.gpsimd.tensor_tensor(out=gated[u][:], in0=z_rows[:], in1=drop[u][:], op=ALU.mult)
+            nc.vector.tensor_tensor(out=gated[u][:], in0=gate_rows[u][:], in1=drop[u][:], op=ALU.mult)
 
         def mix_out(u):
             t, half = divmod(u, HALVES)

from contextlib import ExitStack

import concourse.mybir as mybir
from concourse.masks import make_identity

F32 = mybir.dt.float32
BF16 = mybir.dt.bfloat16
U32 = mybir.dt.uint32
U8 = mybir.dt.uint8
FP8X4 = mybir.dt.float8_e4m3fn_x4
ACT = mybir.ActivationFunctionType
ALU = mybir.AluOpType

P = 128
PACK = 4
BATCH, HIDDEN, RANK = 1024, 2048, 512
WORD_HALVES = 2
STREAMS = 2
ROWS_PER_PARTITION = BATCH // P
HALF_CHUNKS = 4
HALVES = ROWS_PER_PARTITION // HALF_CHUNKS
HIDDEN_TILES = HIDDEN // P
WEIGHT_LOAD_TILES = 2
STATE_LOAD_TILES = 4
UNITS = HIDDEN_TILES * HALVES
TILES_AHEAD = 2
OUT_LAG = 2

FLOPS = 2 * BATCH * HIDDEN * RANK * STREAMS


def tile_fastgrnncudacell_pa_kernel(
    tc, wx_r, uh_r, state, W2, U2, bias_gate, bias_update, zeta, nu, out
):
    nc = tc.nc
    assert tuple(wx_r.shape) == (BATCH, RANK) and tuple(W2.shape) == (HIDDEN, RANK)

    act_views = [x.rearrange("(r i) k -> r i k", i=ROWS_PER_PARTITION) for x in (wx_r, uh_r)]
    state_view = state.rearrange("(r i) d -> r i d", i=ROWS_PER_PARTITION)
    out_view = out.rearrange("(r i) d -> r i d", i=ROWS_PER_PARTITION)
    weight_views = [w.rearrange("(t m) k -> m t k", m=P) for w in (W2, U2)]

    with ExitStack() as ctx:
        ctx.enter_context(tc.manual_schedule())
        keep = ctx.enter_context(tc.tile_pool(name="keep", bufs=1))
        stage = ctx.enter_context(tc.tile_pool(name="stage", bufs=6))
        gates_pool = ctx.enter_context(tc.tile_pool(name="gates", bufs=3))
        mix_pool = ctx.enter_context(tc.tile_pool(name="mix", bufs=4))
        out_pool = ctx.enter_context(tc.tile_pool(name="outs", bufs=6))
        banks = ctx.enter_context(tc.psum_pool(name="banks", bufs=8))

        identity = keep.tile([P, P], F32, name="identity")
        make_identity(nc, identity[:])

        bias_rows = keep.tile([P, P], BF16, name="bias_rows")
        nc.vector.memset(bias_rows[:], 0.0)
        for n, bias in enumerate((bias_gate, bias_update)):
            nc.scalar.dma_start(
                out=bias_rows[n * HIDDEN_TILES : (n + 1) * HIDDEN_TILES, :],
                in_=bias.rearrange("o (t m) -> (o t) m", m=P),
            )
        zeta_col = keep.tile([P, 1], BF16, name="zeta_col")
        nu_col = keep.tile([P, 1], BF16, name="nu_col")
        nc.scalar.dma_start(out=zeta_col[:], in_=zeta.to_broadcast([P, 1]))
        nc.scalar.dma_start(out=nu_col[:], in_=nu.to_broadcast([P, 1]))

        act_raw = {}
        weight_raw = {}
        state_sb = {}

        def load_acts(half):
            for s in range(STREAMS):
                raw = keep.tile([P, HALF_CHUNKS, RANK], BF16, name="act_raw_%d_%d" % (s, half))
                chunks = slice(half * HALF_CHUNKS, (half + 1) * HALF_CHUNKS)
                nc.sync.dma_start(out=raw[:], in_=act_views[s][:, chunks, :])
                act_raw[(s, half)] = raw

        def load_weights(n):
            for s in range(STREAMS):
                raw = keep.tile([P, WEIGHT_LOAD_TILES, RANK], BF16, name="weight_raw_%d_%d" % (s, n))
                tiles = slice(n * WEIGHT_LOAD_TILES, (n + 1) * WEIGHT_LOAD_TILES)
                nc.sync.dma_start(out=raw[:], in_=weight_views[s][:, tiles, :])
                weight_raw[(s, n)] = raw

        def load_state(n):
            part = keep.tile([P, ROWS_PER_PARTITION, STATE_LOAD_TILES * P], BF16, name="state_%d" % n)
            cols = slice(n * STATE_LOAD_TILES * P, (n + 1) * STATE_LOAD_TILES * P)
            nc.sync.dma_start(out=part[:], in_=state_view[:, :, cols])
            state_sb[n] = part

        load_acts(0)
        load_weights(0)
        load_acts(1)
        load_state(0)
        load_weights(1)
        for n in range(1, HIDDEN_TILES // STATE_LOAD_TILES):
            load_weights(2 * n)
            load_weights(2 * n + 1)
            load_state(n)

        sig_zeta = keep.tile([P, 1], F32, name="sig_zeta")
        sig_nu = keep.tile([P, 1], F32, name="sig_nu")
        nc.scalar.activation(out=sig_zeta[:], in_=zeta_col[:], func=ACT.Sigmoid)
        nc.scalar.activation(out=sig_nu[:], in_=nu_col[:], func=ACT.Sigmoid)

        act_codes = [keep.tile([P, BATCH], U32, name="act_codes_%d" % s, align_bytes=64) for s in range(STREAMS)]
        act_scales = [keep.tile([P, BATCH], U8, name="act_scales_%d" % s, align_bytes=64) for s in range(STREAMS)]
        weight_codes = keep.tile([P, STREAMS * HIDDEN], U32, name="weight_codes", align_bytes=64)
        weight_scales = keep.tile([P, STREAMS * HIDDEN], U8, name="weight_scales", align_bytes=64)

        def turn_rows(row_tiles, copy):
            turned = banks.tile([P, WORD_HALVES, 2 * P], F32, tag="bank")
            for n, rows in enumerate(row_tiles):
                words = rows.bitcast(F32)
                for h in range(WORD_HALVES):
                    nc.tensor.transpose(
                        turned[:, h, n * P : (n + 1) * P], words[:, h * P : (h + 1) * P], identity[:]
                    )
            grouped = stage.tile([P, 2 * P, PACK], BF16, align_bytes=64)
            copy(out=grouped[:].bitcast(F32), in_=turned[:].rearrange("p h r -> p r h"))
            return grouped

        def quantise(grouped, codes, scales):
            nc.vector.quantize_mx(
                out=codes.bitcast(FP8X4), scales=scales, in_=grouped[:].rearrange("p r t -> p (r t)")
            )

        def quantise_acts(half):
            grouped = {}
            for s, copy in enumerate((nc.vector.tensor_copy, nc.scalar.copy)):
                for pair in range(HALF_CHUNKS // 2):
                    raw = act_raw[(s, half)]
                    grouped[(s, pair)] = turn_rows([raw[:, 2 * pair, :], raw[:, 2 * pair + 1, :]], copy)
            for s in range(STREAMS):
                for pair in range(HALF_CHUNKS // 2):
                    first = (half * HALF_CHUNKS + 2 * pair) * P
                    cols = slice(first, first + 2 * P)
                    quantise(grouped[(s, pair)], act_codes[s][:, cols], act_scales[s][:, cols])

        def turn_weights(t):
            n, member = divmod(t, WEIGHT_LOAD_TILES)
            return turn_rows([weight_raw[(s, n)][:, member, :] for s in range(STREAMS)], nc.scalar.copy)

        def quantise_weights(t, grouped):
            cols = slice(t * STREAMS * P, (t + 1) * STREAMS * P)
            quantise(grouped, weight_codes[:, cols], weight_scales[:, cols])

        pre = {}
        cand = {}
        gate = {}
        cand_rows = {}
        gate_rows = {}
        drop = {}
        gated = {}

        def products(u):
            t, half = divmod(u, HALVES)
            pre[u] = banks.tile([P, HALF_CHUNKS * P], F32, name="pre", tag="bank")
            b_cols = slice(half * HALF_CHUNKS * P, (half + 1) * HALF_CHUNKS * P)
            for s in range(STREAMS):
                w_cols = slice((t * STREAMS + s) * P, (t * STREAMS + s + 1) * P)
                nc.tensor.matmul_mx(
                    out=pre[u][:],
                    lhsT=weight_codes[:, w_cols].bitcast(FP8X4),
                    lhsT_scale=weight_scales[:, w_cols],
                    rhs=act_codes[s][:, b_cols].bitcast(FP8X4),
                    rhs_scale=act_scales[s][:, b_cols],
                    start=(s == 0),
                    stop=(s == STREAMS - 1),
                )

        def gates(u):
            t = u // HALVES
            cand[u] = gates_pool.tile([P, HALF_CHUNKS * P], F32, name="cand")
            gate[u] = gates_pool.tile([P, HALF_CHUNKS * P], F32, name="gate")
            nc.scalar.activation(
                out=cand[u][:], in_=pre[u][:], func=ACT.Tanh,
                bias=bias_cols[:, HIDDEN_TILES + t : HIDDEN_TILES + t + 1], scale=1.0,
            )
            nc.scalar.activation(
                out=gate[u][:], in_=pre[u][:], func=ACT.Sigmoid, bias=bias_cols[:, t : t + 1], scale=1.0
            )

        def turn_back(u):
            cand_rows[u] = banks.tile([P, HALF_CHUNKS, P], F32, name="cand_rows", tag="bank")
            gate_rows[u] = banks.tile([P, HALF_CHUNKS, P], F32, name="gate_rows", tag="bank")
            for turned, source in ((cand_rows[u], cand[u]), (gate_rows[u], gate[u])):
                for i in range(HALF_CHUNKS):
                    nc.tensor.transpose(turned[:, i, :], source[:, i * P : (i + 1) * P], identity[:])

        def mix_drop(u):
            t, half = divmod(u, HALVES)
            n, member = divmod(t, STATE_LOAD_TILES)
            chunks = slice(half * HALF_CHUNKS, (half + 1) * HALF_CHUNKS)
            drop[u] = mix_pool.tile([P, HALF_CHUNKS, P], F32, name="drop")
            nc.vector.scalar_tensor_tensor(
                out=drop[u][:], in0=cand_rows[u][:], scalar=sig_zeta[:, 0:1],
                in1=state_sb[n][:, chunks, member * P : (member + 1) * P],
                op0=ALU.mult, op1=ALU.subtract,
            )

        def mix_gate(u):
            gated[u] = mix_pool.tile([P, HALF_CHUNKS, P], F32, name="gated")
            nc.vector.tensor_tensor(out=gated[u][:], in0=gate_rows[u][:], in1=drop[u][:], op=ALU.mult)

        def mix_out(u):
            t, half = divmod(u, HALVES)
            chunks = slice(half * HALF_CHUNKS, (half + 1) * HALF_CHUNKS)
            out_tile = out_pool.tile([P, HALF_CHUNKS, P], F32, name="out_tile")
            nc.vector.scalar_tensor_tensor(
                out=out_tile[:], in0=cand_rows[u][:], scalar=sig_sum[:, 0:1], in1=gated[u][:],
                op0=ALU.mult, op1=ALU.subtract,
            )
            nc.sync.dma_start(out=out_view[:, chunks, t * P : (t + 1) * P], in_=out_tile[:])

        quantise_acts(0)
        quantise_weights(0, turn_weights(0))

        bias_rows_f32 = keep.tile([P, P], F32, name="bias_rows_f32")
        nc.vector.tensor_copy(out=bias_rows_f32[:], in_=bias_rows[:])
        bias_turned = banks.tile([P, P], F32, tag="bank")
        nc.tensor.transpose(bias_turned[:], bias_rows_f32[:], identity[:])
        bias_cols = keep.tile([P, 2 * HIDDEN_TILES], F32, name="bias_cols")
        nc.vector.tensor_copy(out=bias_cols[:], in_=bias_turned[:, 0 : 2 * HIDDEN_TILES])
        sig_sum = keep.tile([P, 1], F32, name="sig_sum")
        nc.vector.tensor_add(out=sig_sum[:], in0=sig_zeta[:], in1=sig_nu[:])

        products(0)
        gates(0)
        quantise_acts(1)
        quantise_weights(1, turn_weights(1))

        grouped_ahead = {}
        for u in range(UNITS + OUT_LAG):
            t_ahead = u // HALVES + TILES_AHEAD
            if u + 1 < UNITS:
                products(u + 1)
                gates(u + 1)
            if u < UNITS:
                turn_back(u)
                if u % HALVES == 0 and t_ahead < HIDDEN_TILES:
                    grouped_ahead[t_ahead] = turn_weights(t_ahead)
                mix_drop(u)
            if u >= OUT_LAG:
                mix_out(u - OUT_LAG)
            if u < UNITS:
                mix_gate(u)
                if u % HALVES == 1 and t_ahead < HIDDEN_TILES:
                    quantise_weights(t_ahead, grouped_ahead[t_ahead])
